import numpy as np
import ml_dtypes


def mxq(x, axis, fmt="e4m3"):
    dtype, down = {"e4m3": (ml_dtypes.float8_e4m3fn, 7), "e5m2": (ml_dtypes.float8_e5m2, 14)}[fmt]
    v = np.moveaxis(np.asarray(x, np.float32).astype(ml_dtypes.bfloat16).astype(np.float64), axis, -1)
    blocks = v.reshape(v.shape[:-1] + (-1, 32))
    amax = np.abs(blocks).max(-1, keepdims=True)
    byte = np.maximum(np.where(amax > 0, np.frexp(amax)[1] - 1 + 127, 0) - down, 1)
    scale = np.exp2(byte - 127.0)
    codes = (blocks / scale).astype(np.float32).astype(dtype).astype(np.float64)
    return np.moveaxis((codes * scale).reshape(v.shape), -1, axis)


WIDE = False


def mx_kscale(k):
    if not WIDE:
        return np.ones(k)
    levels = np.array([10, -10, 5, -5, 0])
    a = np.random.permutation(np.resize(levels, k // 512 * 4)).reshape(k // 512, 4)
    idx = np.arange(k)
    return np.exp2(a[idx // 512, idx % 128 // 32])


BF16 = ml_dtypes.bfloat16


def bf(x):
    return np.asarray(x, np.float32).astype(BF16)


def f64(x):
    return np.asarray(x).astype(np.float64)


B, SQ, SK, D, DV = 8, 2048, 1024, 128, 128


def setup_inputs():
    t = mx_kscale(SK)
    return {"qk": bf(1.0 + 0.1 * np.random.standard_normal((1, 1))),
            "qk_scaling_factor": bf(1.5 + 0.1 * np.random.standard_normal((1, 1))),
            "query": bf(np.random.standard_normal((B, SQ, D))),
            "key": bf(np.random.standard_normal((B, SK, D)) * t[:, None]),
            "value": bf(np.random.standard_normal((B, SK, DV)) * 1.5 / np.sqrt(SK) / t[:, None])}


def reference(qk, qk_scaling_factor, query, key, value):
    gain = np.sqrt(D)
    scores = f64(query) @ f64(key).transpose(0, 2, 1)
    scores = scores / gain
    scores = scores / f64(qk_scaling_factor)
    scores = scores
    return mxq(scores, 2, "e4m3") @ mxq(f64(value), 1, "e4m3")

@@ -1,0 +1,247 @@
+from contextlib import ExitStack
+import math
+
+import concourse.bass as bass
+import concourse.mybir as mybir
+import concourse.tile as tile
+from concourse.masks import make_identity
+
+B = 8
+SQ = 2048
+SK = 1024
+D = 128
+DV = 128
+FLOPS = 2 * B * SQ * SK * D + 2 * B * SQ * SK * DV
+
+P = 128
+PACK = 4
+PASSES = SK // (P * PACK)
+QBLOCKS = SQ // P
+QGROUP = 4
+UNITS = B * (QBLOCKS // QGROUP) * PASSES
+UNITS_PER_BATCH = UNITS // B
+
+BF16 = mybir.dt.bfloat16
+F32 = mybir.dt.float32
+U32 = mybir.dt.uint32
+U8 = mybir.dt.uint8
+FP8X4 = mybir.dt.float8_e4m3fn_x4
+COPY = mybir.ActivationFunctionType.Copy
+MULT = mybir.AluOpType.mult
+
+PIN = True
+NSC = 6
+MXLAG = 4
+VB = (0,)
+WEAVE = False
+TR_ENG = ('V','V','V')
+TR_ENG0 = ('V','S','S')
+
+
+def tile_model_kernel(tc, qk, qk_scaling_factor, query, key, value, out):
+    nc = tc.nc
+    with ExitStack() as ctx:
+        if PIN:
+            ctx.enter_context(tc.manual_schedule())
+        const = ctx.enter_context(tc.tile_pool(name="const", bufs=1))
+        inp = ctx.enter_context(tc.tile_pool(name="inp", bufs=1))
+        tpool = ctx.enter_context(tc.tile_pool(name="tpool", bufs=2))
+        vpool = ctx.enter_context(tc.tile_pool(name="vpool", bufs=3))
+        gpool = ctx.enter_context(tc.tile_pool(name="gpool", bufs=4))
+        cpool = ctx.enter_context(tc.tile_pool(name="cpool", bufs=6))
+        opool = ctx.enter_context(tc.tile_pool(name="opool", bufs=4))
+        psc = ctx.enter_context(tc.psum_pool(name="psc", bufs=NSC))
+        pso = ctx.enter_context(tc.psum_pool(name="pso", bufs=1))
+        ptr = ctx.enter_context(tc.psum_pool(name="ptr", bufs=1))
+
+        key_sb, query_sb, value_sb = [], [], []
+        for b in range(B):
+            key_sb.append(inp.tile([P, PASSES, PACK, D], BF16, name="key_sb%d" % b))
+            query_sb.append(inp.tile([P, QBLOCKS, D], BF16, name="query_sb%d" % b))
+            value_sb.append(inp.tile([P, PASSES, PACK, DV], BF16, name="value_sb%d" % b))
+        sf_raw = const.tile([P, 1], BF16, name="sf_raw")
+
+        def load_key(b):
+            nc.sync.dma_start(
+                out=key_sb[b][:],
+                in_=key[b].rearrange("(c p t) d -> p c t d", c=PASSES, p=P, t=PACK),
+            )
+
+        def load_value(b):
+            nc.sync.dma_start(
+                out=value_sb[b][:],
+                in_=value[b].rearrange("(c p t) d -> p c t d", c=PASSES, p=P, t=PACK),
+            )
+
+        def load_query(b, lo, hi):
+            nc.sync.dma_start(
+                out=query_sb[b][:, lo:hi, :],
+                in_=query[b].rearrange("(p j) d -> p j d", j=QBLOCKS)[:, lo:hi, :],
+            )
+
+        load_key(0)
+        load_query(0, 0, QBLOCKS // 2)
+        nc.scalar.dma_start(
+            out=sf_raw[:],
+            in_=qk_scaling_factor.rearrange("a b -> (a b)").partition_broadcast(P),
+        )
+        load_value(0)
+        load_query(0, QBLOCKS // 2, QBLOCKS)
+        for b in range(1, B):
+            load_key(b)
+            load_query(b, 0, QBLOCKS)
+            load_value(b)
+
+        ident = const.tile([P, P], BF16, name="ident")
+        make_identity(nc, ident[:])
+
+        keyT, queryT, vcodes, vscales = {}, {}, {}, {}
+
+        def copy_on(eng, dst, src):
+            if eng == "V":
+                nc.vector.tensor_copy(out=dst, in_=src)
+            else:
+                nc.scalar.copy(out=dst, in_=src)
+
+        def transposes(b, part, eng, head):
+            if head:
+                bank = psc.tile([P, 8, P], BF16, name="trh", tag="sc")
+            else:
+                bank = ptr.tile([P, 8, P], BF16, name="tr", tag="tr")
+            steps = []
+            if part == 0:
+                keyT[b] = tpool.tile([P, PASSES * PACK, P], BF16, name="keyT", tag="keyT")
+                for i in range(8):
+                    steps.append((bank[:, i, :], key_sb[b][:, i // PACK, i % PACK, :]))
+                dst = keyT[b][:]
+            else:
+                if part == 1:
+                    queryT[b] = tpool.tile([P, QBLOCKS, P], BF16, name="queryT", tag="queryT")
+                lo = 8 * (part - 1)
+                for i in range(8):
+                    steps.append((bank[:, i, :], query_sb[b][:, lo + i, :]))
+                dst = queryT[b][:, lo : lo + 8, :]
+            return steps, (eng, dst, bank[:])
+
+        def run_transposes(job):
+            steps, fin = job
+            for dst, src in steps:
+                nc.tensor.transpose(out=dst, in_=src, identity=ident[:])
+            copy_on(*fin)
+
+        def value_prep(b):
+            vgrp = vpool.tile([P, PASSES, DV, PACK], BF16, name="vgrp", tag="vgrp", align_bytes=64)
+            nc.vector.tensor_copy(
+                out=vgrp[:], in_=value_sb[b][:].rearrange("p c t w -> p c w t")
+            )
+            vcodes[b] = vpool.tile([P, PASSES, DV], U32, name="vcodes", tag="vcodes", align_bytes=64)
+            vscales[b] = vpool.tile([P, PASSES, DV], U8, name="vscales", tag="vscales", align_bytes=64)
+            return vgrp
+
+        def value_quant(b, vgrp):
+            nc.vector.quantize_mx(
+                out=vcodes[b][:].rearrange("p c w -> p (c w)").bitcast(FP8X4),
+                scales=vscales[b][:].rearrange("p c w -> p (c w)"),
+                in_=vgrp[:].rearrange("p c w t -> p (c w t)"),
+            )
+
+        run_transposes(transposes(0, 0, TR_ENG0[0], True))
+        run_transposes(transposes(0, 1, TR_ENG0[1], True))
+
+        sf_gain = const.tile([P, 1], F32, name="sf_gain")
+        inv = const.tile([P, 1], F32, name="inv")
+        nc.vector.tensor_scalar(
+            out=sf_gain[:], in0=sf_raw[:], scalar1=math.sqrt(D), scalar2=None, op0=MULT
+        )
+        nc.vector.reciprocal(out=inv[:], in_=sf_gain[:])
+
+
+        grp, codes, scl, obank = {}, {}, {}, {}
+        pending_out = []
+        pending_vq = []
+
+        for u in range(UNITS + MXLAG + 2):
+            if u < UNITS:
+                b = u // UNITS_PER_BATCH
+                r = u % UNITS_PER_BATCH
+                g = r // PASSES
+                c = r % PASSES
+                job = None
+                if u == 1:
+                    job = transposes(0, 2, TR_ENG0[2], False)
+                elif b + 1 < B and r in (2, 4, 6):
+                    job = transposes(b + 1, r // 2 - 1, TR_ENG[r // 2 - 1], False)
+                banks = []
+                for jj in range(QGROUP):
+                    sc = psc.tile([P, PACK, P], F32, name="sc", tag="sc")
+                    banks.append(sc)
+                    for t in range(PACK):
+                        nc.tensor.matmul(
+                            out=sc[:, t, :],
+                            lhsT=keyT[b][:, PACK * c + t, :],
+                            rhs=queryT[b][:, QGROUP * g + jj, :],
+                            start=True,
+                            stop=True,
+                        )
+                        if WEAVE and job is not None and jj in (1, 2):
+                            dst, src = job[0][(jj - 1) * PACK + t]
+                            nc.tensor.transpose(out=dst, in_=src, identity=ident[:])
+                    if job is not None and not WEAVE and jj == 1:
+                        run_transposes(job)
+                    if job is not None and WEAVE and jj == 2:
+                        copy_on(*job[1])
+                grp[u] = gpool.tile([P, QGROUP, P, PACK], BF16, name="grp", tag="grp", align_bytes=64)
+                for jj in range(QGROUP):
+                    src = banks[jj][:].rearrange("p t q -> p q t")
+                    if jj in VB:
+                        nc.vector.tensor_scalar(
+                            out=grp[u][:, jj, :, :], in0=src, scalar1=inv[:, 0:1], scalar2=None, op0=MULT
+                        )
+                    else:
+                        nc.scalar.activation(out=grp[u][:, jj, :, :], in_=src, func=COPY, scale=inv[:, 0:1])
+                if u == 0:
+                    pending_vq.append((0, value_prep(0)))
+                elif r == 3 and b + 1 < B:
+                    pending_vq.append((b + 1, value_prep(b + 1)))
+
+            for G in pending_out:
+                osb = opool.tile([P, QGROUP, DV], F32, name="osb", tag="osb")
+                nc.vector.tensor_copy(out=osb[:], in_=obank[G][:])
+                gb, gg = G // (QBLOCKS // QGROUP), G % (QBLOCKS // QGROUP)
+                nc.sync.dma_start(
+                    out=out[gb].rearrange("(p j) d -> p j d", j=QBLOCKS)[:, QGROUP * gg : QGROUP * (gg + 1), :],
+                    in_=osb[:],
+                )
+            pending_out = []
+
+            if 1 <= u <= UNITS:
+                q = u - 1
+                codes[q] = cpool.tile([P, QGROUP * P], U32, name="codes", tag="codes", align_bytes=64)
+                scl[q] = cpool.tile([P, QGROUP * P], U8, name="scl", tag="scl", align_bytes=64)
+                nc.vector.quantize_mx(
+                    out=codes[q][:].bitcast(FP8X4),
+                    scales=scl[q][:],
+                    in_=grp[q][:].rearrange("p j q t -> p (j q t)"),
+                )
+            for vb, vgrp in pending_vq:
+                value_quant(vb, vgrp)
+            pending_vq = []
+
+            uu = u - MXLAG
+            if uu >= 0 and uu % PASSES == 0 and uu < UNITS:
+                G = uu // PASSES
+                gb = G // (QBLOCKS // QGROUP)
+                obank[G] = pso.tile([P, QGROUP, DV], F32, name="ob", tag="ob")
+                for jj in range(QGROUP):
+                    cols = slice(jj * P, (jj + 1) * P)
+                    for c in range(PASSES):
+                        nc.tensor.matmul_mx(
+                            out=obank[G][:, jj, :],
+                            lhsT=codes[uu + c][:, cols].bitcast(FP8X4),
+                            lhsT_scale=scl[uu + c][:, cols],
+                            rhs=vcodes[gb][:, c, :].bitcast(FP8X4),
+                            rhs_scale=vscales[gb][:, c, :],
+                            start=(c == 0),
+                            stop=(c == PASSES - 1),
+                        )
+                pending_out.append(G)

@@ -1,9 +1,7 @@
 from contextlib import ExitStack
 import math
 
-import concourse.bass as bass
 import concourse.mybir as mybir
-import concourse.tile as tile
 from concourse.masks import make_identity
 
 B = 8
@@ -18,7 +16,8 @@ PACK = 4
 PASSES = SK // (P * PACK)
 QBLOCKS = SQ // P
 QGROUP = 4
-UNITS = B * (QBLOCKS // QGROUP) * PASSES
+GROUPS = QBLOCKS // QGROUP
+UNITS = B * GROUPS * PASSES
 UNITS_PER_BATCH = UNITS // B
 
 BF16 = mybir.dt.bfloat16
@@ -32,10 +31,11 @@ MULT = mybir.AluOpType.mult
 PIN = True
 NSC = 6
 MXLAG = 4
-VB = (0,)
-WEAVE = False
-TR_ENG = ('V','V','V')
-TR_ENG0 = ('V','S','S')
+K1 = 2
+OUT_S_FROM = 30
+TAIL_FINE = 1
+WEAVE = True
+JOB_AT = (2, 4, 6)
 
 
 def tile_model_kernel(tc, qk, qk_scaling_factor, query, key, value, out):
@@ -47,8 +47,8 @@ def tile_model_kernel(tc, qk, qk_scaling_factor, query, key, value, out):
         inp = ctx.enter_context(tc.tile_pool(name="inp", bufs=1))
         tpool = ctx.enter_context(tc.tile_pool(name="tpool", bufs=2))
         vpool = ctx.enter_context(tc.tile_pool(name="vpool", bufs=3))
-        gpool = ctx.enter_context(tc.tile_pool(name="gpool", bufs=4))
-        cpool = ctx.enter_context(tc.tile_pool(name="cpool", bufs=6))
+        gpool = ctx.enter_context(tc.tile_pool(name="gpool", bufs=6))
+        cpool = ctx.enter_context(tc.tile_pool(name="cpool", bufs=8))
         opool = ctx.enter_context(tc.tile_pool(name="opool", bufs=4))
         psc = ctx.enter_context(tc.psum_pool(name="psc", bufs=NSC))
         pso = ctx.enter_context(tc.psum_pool(name="pso", bufs=1))
@@ -61,10 +61,10 @@ def tile_model_kernel(tc, qk, qk_scaling_factor, query, key, value, out):
             value_sb.append(inp.tile([P, PASSES, PACK, DV], BF16, name="value_sb%d" % b))
         sf_raw = const.tile([P, 1], BF16, name="sf_raw")
 
-        def load_key(b):
+        def load_key(b, lo, hi):
             nc.sync.dma_start(
-                out=key_sb[b][:],
-                in_=key[b].rearrange("(c p t) d -> p c t d", c=PASSES, p=P, t=PACK),
+                out=key_sb[b][:, lo:hi, :, :],
+                in_=key[b].rearrange("(c p t) d -> p c t d", c=PASSES, p=P, t=PACK)[:, lo:hi, :, :],
             )
 
         def load_value(b):
@@ -79,16 +79,18 @@ def tile_model_kernel(tc, qk, qk_scaling_factor, query, key, value, out):
                 in_=query[b].rearrange("(p j) d -> p j d", j=QBLOCKS)[:, lo:hi, :],
             )
 
-        load_key(0)
-        load_query(0, 0, QBLOCKS // 2)
         nc.scalar.dma_start(
             out=sf_raw[:],
             in_=qk_scaling_factor.rearrange("a b -> (a b)").partition_broadcast(P),
         )
+        load_key(0, 0, 1)
+        load_query(0, 0, 4)
+        load_key(0, 1, 2)
         load_value(0)
-        load_query(0, QBLOCKS // 2, QBLOCKS)
+        load_query(0, 4, 8)
+        load_query(0, 8, 16)
         for b in range(1, B):
-            load_key(b)
+            load_key(b, 0, PASSES)
             load_query(b, 0, QBLOCKS)
             load_value(b)
 
@@ -103,62 +105,67 @@ def tile_model_kernel(tc, qk, qk_scaling_factor, query, key, value, out):
             else:
                 nc.scalar.copy(out=dst, in_=src)
 
-        def transposes(b, part, eng, head):
+        def tr_job(kind, b, lo, hi, eng, head):
             if head:
                 bank = psc.tile([P, 8, P], BF16, name="trh", tag="sc")
             else:
                 bank = ptr.tile([P, 8, P], BF16, name="tr", tag="tr")
             steps = []
-            if part == 0:
-                keyT[b] = tpool.tile([P, PASSES * PACK, P], BF16, name="keyT", tag="keyT")
-                for i in range(8):
-                    steps.append((bank[:, i, :], key_sb[b][:, i // PACK, i % PACK, :]))
-                dst = keyT[b][:]
+            for i in range(lo, hi):
+                if kind == "k":
+                    steps.append((bank[:, i - lo, :], key_sb[b][:, i // PACK, i % PACK, :]))
+                else:
+                    steps.append((bank[:, i - lo, :], query_sb[b][:, i, :]))
+            if kind == "k":
+                dst = keyT[b][:, lo:hi, :]
             else:
-                if part == 1:
-                    queryT[b] = tpool.tile([P, QBLOCKS, P], BF16, name="queryT", tag="queryT")
-                lo = 8 * (part - 1)
-                for i in range(8):
-                    steps.append((bank[:, i, :], query_sb[b][:, lo + i, :]))
-                dst = queryT[b][:, lo : lo + 8, :]
-            return steps, (eng, dst, bank[:])
+                dst = queryT[b][:, lo:hi, :]
+            return steps, (eng, dst, bank[:, 0 : hi - lo, :])
 
-        def run_transposes(job):
-            steps, fin = job
-            for dst, src in steps:
-                nc.tensor.transpose(out=dst, in_=src, identity=ident[:])
-            copy_on(*fin)
+        def new_transposed(b):
+            keyT[b] = tpool.tile([P, PASSES * PACK, P], BF16, name="keyT", tag="keyT")
+            queryT[b] = tpool.tile([P, QBLOCKS, P], BF16, name="queryT", tag="queryT")
 
-        def value_prep(b):
+        def one_transpose(step):
+            nc.tensor.transpose(out=step[0], in_=step[1], identity=ident[:])
+
+        def value_regroup(b):
             vgrp = vpool.tile([P, PASSES, DV, PACK], BF16, name="vgrp", tag="vgrp", align_bytes=64)
             nc.vector.tensor_copy(
                 out=vgrp[:], in_=value_sb[b][:].rearrange("p c t w -> p c w t")
             )
-            vcodes[b] = vpool.tile([P, PASSES, DV], U32, name="vcodes", tag="vcodes", align_bytes=64)
-            vscales[b] = vpool.tile([P, PASSES, DV], U8, name="vscales", tag="vscales", align_bytes=64)
             return vgrp
 
         def value_quant(b, vgrp):
+            vcodes[b] = vpool.tile([P, PASSES, DV], U32, name="vcodes", tag="vcodes", align_bytes=64)
+            vscales[b] = vpool.tile([P, PASSES, DV], U8, name="vscales", tag="vscales", align_bytes=64)
             nc.vector.quantize_mx(
                 out=vcodes[b][:].rearrange("p c w -> p (c w)").bitcast(FP8X4),
                 scales=vscales[b][:].rearrange("p c w -> p (c w)"),
                 in_=vgrp[:].rearrange("p c w t -> p (c w t)"),
             )
 
-        run_transposes(transposes(0, 0, TR_ENG0[0], True))
-        run_transposes(transposes(0, 1, TR_ENG0[1], True))
-
+        new_transposed(0)
         sf_gain = const.tile([P, 1], F32, name="sf_gain")
         inv = const.tile([P, 1], F32, name="inv")
-        nc.vector.tensor_scalar(
-            out=sf_gain[:], in0=sf_raw[:], scalar1=math.sqrt(D), scalar2=None, op0=MULT
+        head_jobs = (
+            tr_job("k", 0, 0, 4, "V", True),
+            tr_job("q", 0, 0, 4, "S", True),
+            tr_job("k", 0, 4, 8, "V", True),
         )
-        nc.vector.reciprocal(out=inv[:], in_=sf_gain[:])
-
+        for n, job in enumerate(head_jobs):
+            for step in job[0]:
+                one_transpose(step)
+            copy_on(*job[1])
+            if n == 0:
+                nc.vector.tensor_scalar(
+                    out=sf_gain[:], in0=sf_raw[:], scalar1=math.sqrt(D), scalar2=None, op0=MULT
+                )
+                nc.vector.reciprocal(out=inv[:], in_=sf_gain[:])
 
         grp, codes, scl, obank = {}, {}, {}, {}
         pending_out = []
-        pending_vq = []
+        pending_vq = [(0, value_regroup(0))]
 
         for u in range(UNITS + MXLAG + 2):
             if u < UNITS:
@@ -167,10 +174,22 @@ def tile_model_kernel(tc, qk, qk_scaling_factor, query, key, value, out):
                 g = r // PASSES
                 c = r % PASSES
                 job = None
-                if u == 1:
-                    job = transposes(0, 2, TR_ENG0[2], False)
-                elif b + 1 < B and r in (2, 4, 6):
-                    job = transposes(b + 1, r // 2 - 1, TR_ENG[r // 2 - 1], False)
+                if u == 0:
+                    job = tr_job("q", 0, 4, 8, "S", False)
+                elif u == 1:
+                    job = tr_job("q", 0, 8, 16, "S", False)
+                elif b + 1 < B and r in JOB_AT:
+                    part = JOB_AT.index(r)
+                    eng = "S" if (part == 1 and b % 2 == 1) else "V"
+                    if part == 0:
+                        new_transposed(b + 1)
+                        job = tr_job("k", b + 1, 0, 8, eng, False)
+                    else:
+                        job = tr_job("q", b + 1, 8 * (part - 1), 8 * part, eng, False)
+                todo = []
+                if job is not None:
+                    todo = job[0]
+                done = 0
                 banks = []
                 for jj in range(QGROUP):
                     sc = psc.tile([P, PACK, P], F32, name="sc", tag="sc")
@@ -183,31 +202,31 @@ def tile_model_kernel(tc, qk, qk_scaling_factor, query, key, value, out):
                             start=True,
                             stop=True,
                         )
-                        if WEAVE and job is not None and jj in (1, 2):
-                            dst, src = job[0][(jj - 1) * PACK + t]
-                            nc.tensor.transpose(out=dst, in_=src, identity=ident[:])
-                    if job is not None and not WEAVE and jj == 1:
-                        run_transposes(job)
-                    if job is not None and WEAVE and jj == 2:
-                        copy_on(*job[1])
+                        if WEAVE and jj in (1, 2) and done < len(todo):
+                            one_transpose(todo[done])
+                            done += 1
+                    if not WEAVE and jj == 1:
+                        for step in todo:
+                            one_transpose(step)
                 grp[u] = gpool.tile([P, QGROUP, P, PACK], BF16, name="grp", tag="grp", align_bytes=64)
+                on_vector = (0, 2) if u < K1 else (0,)
                 for jj in range(QGROUP):
                     src = banks[jj][:].rearrange("p t q -> p q t")
-                    if jj in VB:
+                    if jj in on_vector:
                         nc.vector.tensor_scalar(
                             out=grp[u][:, jj, :, :], in0=src, scalar1=inv[:, 0:1], scalar2=None, op0=MULT
                         )
                     else:
                         nc.scalar.activation(out=grp[u][:, jj, :, :], in_=src, func=COPY, scale=inv[:, 0:1])
-                if u == 0:
-                    pending_vq.append((0, value_prep(0)))
-                elif r == 3 and b + 1 < B:
-                    pending_vq.append((b + 1, value_prep(b + 1)))
+                if job is not None:
+                    copy_on(*job[1])
+                if r == 3 and b + 1 < B:
+                    pending_vq.append((b + 1, value_regroup(b + 1)))
 
             for G in pending_out:
                 osb = opool.tile([P, QGROUP, DV], F32, name="osb", tag="osb")
-                nc.vector.tensor_copy(out=osb[:], in_=obank[G][:])
-                gb, gg = G // (QBLOCKS // QGROUP), G % (QBLOCKS // QGROUP)
+                copy_on("S" if G >= OUT_S_FROM else "V", osb[:], obank[G][:])
+                gb, gg = G // GROUPS, G % GROUPS
                 nc.sync.dma_start(
                     out=out[gb].rearrange("(p j) d -> p j d", j=QBLOCKS)[:, QGROUP * gg : QGROUP * (gg + 1), :],
                     in_=osb[:],
@@ -218,11 +237,15 @@ def tile_model_kernel(tc, qk, qk_scaling_factor, query, key, value, out):
                 q = u - 1
                 codes[q] = cpool.tile([P, QGROUP * P], U32, name="codes", tag="codes", align_bytes=64)
                 scl[q] = cpool.tile([P, QGROUP * P], U8, name="scl", tag="scl", align_bytes=64)
-                nc.vector.quantize_mx(
-                    out=codes[q][:].bitcast(FP8X4),
-                    scales=scl[q][:],
-                    in_=grp[q][:].rearrange("p j q t -> p (j q t)"),
-                )
+                pieces = QGROUP if q >= UNITS - TAIL_FINE else 1
+                width = QGROUP * P // pieces
+                for i in range(pieces):
+                    cols = slice(i * width, (i + 1) * width)
+                    nc.vector.quantize_mx(
+                        out=codes[q][:, cols].bitcast(FP8X4),
+                        scales=scl[q][:, cols],
+                        in_=grp[q][:].rearrange("p j q t -> p (j q t)")[:, i * width * PACK : (i + 1) * width * PACK],
+                    )
             for vb, vgrp in pending_vq:
                 value_quant(vb, vgrp)
             pending_vq = []
@@ -230,7 +253,7 @@ def tile_model_kernel(tc, qk, qk_scaling_factor, query, key, value, out):
             uu = u - MXLAG
             if uu >= 0 and uu % PASSES == 0 and uu < UNITS:
                 G = uu // PASSES
-                gb = G // (QBLOCKS // QGROUP)
+                gb = G // GROUPS
                 obank[G] = pso.tile([P, QGROUP, DV], F32, name="ob", tag="ob")
                 for jj in range(QGROUP):
                     cols = slice(jj * P, (jj + 1) * P)

@@ -35,6 +35,9 @@ K1 = 2
 OUT_S_FROM = 30
 TAIL_FINE = 1
 WEAVE = True
+TRX_POS = 1
+TAIL_SPLIT = True
+WARM = 0
 JOB_AT = (2, 4, 6)
 
 
@@ -163,7 +166,7 @@ def tile_model_kernel(tc, qk, qk_scaling_factor, query, key, value, out):
                 )
                 nc.vector.reciprocal(out=inv[:], in_=sf_gain[:])
 
-        grp, codes, scl, obank = {}, {}, {}, {}
+        grp, codes, scl = {}, {}, {}
         pending_out = []
         pending_vq = [(0, value_regroup(0))]
 
@@ -218,18 +221,18 @@ def tile_model_kernel(tc, qk, qk_scaling_factor, query, key, value, out):
                         )
                     else:
                         nc.scalar.activation(out=grp[u][:, jj, :, :], in_=src, func=COPY, scale=inv[:, 0:1])
-                if job is not None:
-                    copy_on(*job[1])
+                    if job is not None and jj == TRX_POS:
+                        copy_on(*job[1])
                 if r == 3 and b + 1 < B:
                     pending_vq.append((b + 1, value_regroup(b + 1)))
 
-            for G in pending_out:
+            for G, lo, hi, bank, eng in pending_out:
                 osb = opool.tile([P, QGROUP, DV], F32, name="osb", tag="osb")
-                copy_on("S" if G >= OUT_S_FROM else "V", osb[:], obank[G][:])
+                copy_on(eng, osb[:, lo:hi, :], bank[:, lo:hi, :])
                 gb, gg = G // GROUPS, G % GROUPS
                 nc.sync.dma_start(
-                    out=out[gb].rearrange("(p j) d -> p j d", j=QBLOCKS)[:, QGROUP * gg : QGROUP * (gg + 1), :],
-                    in_=osb[:],
+                    out=out[gb].rearrange("(p j) d -> p j d", j=QBLOCKS)[:, QGROUP * gg + lo : QGROUP * gg + hi, :],
+                    in_=osb[:, lo:hi, :],
                 )
             pending_out = []
 
@@ -254,17 +257,25 @@ def tile_model_kernel(tc, qk, qk_scaling_factor, query, key, value, out):
             if uu >= 0 and uu % PASSES == 0 and uu < UNITS:
                 G = uu // PASSES
                 gb = G // GROUPS
-                obank[G] = pso.tile([P, QGROUP, DV], F32, name="ob", tag="ob")
-                for jj in range(QGROUP):
-                    cols = slice(jj * P, (jj + 1) * P)
-                    for c in range(PASSES):
-                        nc.tensor.matmul_mx(
-                            out=obank[G][:, jj, :],
-                            lhsT=codes[uu + c][:, cols].bitcast(FP8X4),
-                            lhsT_scale=scl[uu + c][:, cols],
-                            rhs=vcodes[gb][:, c, :].bitcast(FP8X4),
-                            rhs_scale=vscales[gb][:, c, :],
-                            start=(c == 0),
-                            stop=(c == PASSES - 1),
-                        )
-                pending_out.append(G)
+                if TAIL_SPLIT and G == B * GROUPS - 1:
+                    parts = ((0, QGROUP - 1, "V"), (QGROUP - 1, QGROUP, "S"))
+                else:
+                    parts = ((0, QGROUP, "S" if G >= OUT_S_FROM else "V"),)
+                for lo, hi, eng in parts:
+                    if len(parts) > 1:
+                        bank = psc.tile([P, QGROUP, DV], F32, name="obl", tag="sc")
+                    else:
+                        bank = pso.tile([P, QGROUP, DV], F32, name="ob", tag="ob")
+                    for jj in range(lo, hi):
+                        cols = slice(jj * P, (jj + 1) * P)
+                        for c in range(PASSES):
+                            nc.tensor.matmul_mx(
+                                out=bank[:, jj, :],
+                                lhsT=codes[uu + c][:, cols].bitcast(FP8X4),
+                                lhsT_scale=scl[uu + c][:, cols],
+                                rhs=vcodes[gb][:, c, :].bitcast(FP8X4),
+                                rhs_scale=vscales[gb][:, c, :],
+                                start=(c == 0),
+                                stop=(c == PASSES - 1),
+                            )
+                    pending_out.append((G, lo, hi, bank, eng))

@@ -27,6 +27,7 @@ U8 = mybir.dt.uint8
 FP8X4 = mybir.dt.float8_e4m3fn_x4
 COPY = mybir.ActivationFunctionType.Copy
 MULT = mybir.AluOpType.mult
+ADD = mybir.AluOpType.add
 
 PIN = True
 NSC = 6
@@ -39,6 +40,7 @@ TRX_POS = 1
 TAIL_SPLIT = True
 WARM = 0
 JOB_AT = (2, 4, 6)
+REGROUP = "G"
 
 
 def tile_model_kernel(tc, qk, qk_scaling_factor, query, key, value, out):
@@ -134,9 +136,20 @@ def tile_model_kernel(tc, qk, qk_scaling_factor, query, key, value, out):
 
         def value_regroup(b):
             vgrp = vpool.tile([P, PASSES, DV, PACK], BF16, name="vgrp", tag="vgrp", align_bytes=64)
-            nc.vector.tensor_copy(
-                out=vgrp[:], in_=value_sb[b][:].rearrange("p c t w -> p c w t")
-            )
+            if REGROUP == "G":
+                for c in range(PASSES):
+                    nc.gpsimd.tensor_scalar(
+                        out=vgrp[:, c, :, :],
+                        in0=value_sb[b][:, c, :, :].rearrange("p t w -> p w t"),
+                        scalar1=1.0,
+                        scalar2=0.0,
+                        op0=MULT,
+                        op1=ADD,
+                    )
+            else:
+                nc.vector.tensor_copy(
+                    out=vgrp[:], in_=value_sb[b][:].rearrange("p c t w -> p c w t")
+                )
             return vgrp
 
         def value_quant(b, vgrp):

@@ -35,7 +35,7 @@ MXLAG = 4
 K1 = 2
 OUT_S_FROM = 30
 TAIL_FINE = 1
-WEAVE = True
+WEAVE = False
 TRX_POS = 1
 TAIL_SPLIT = True
 WARM = 0

@@ -40,7 +40,12 @@ TRX_POS = 1
 TAIL_SPLIT = True
 WARM = 0
 JOB_AT = (2, 4, 6)
+JOB_AT_FIRST = (2, 4, 6)
 REGROUP = "G"
+GP_PIECES = 4
+QWIDE = False
+VMUL = "TT"
+V2_EVERY = 10
 
 
 def tile_model_kernel(tc, qk, qk_scaling_factor, query, key, value, out):
@@ -52,8 +57,8 @@ def tile_model_kernel(tc, qk, qk_scaling_factor, query, key, value, out):
         inp = ctx.enter_context(tc.tile_pool(name="inp", bufs=1))
         tpool = ctx.enter_context(tc.tile_pool(name="tpool", bufs=2))
         vpool = ctx.enter_context(tc.tile_pool(name="vpool", bufs=3))
-        gpool = ctx.enter_context(tc.tile_pool(name="gpool", bufs=6))
-        cpool = ctx.enter_context(tc.tile_pool(name="cpool", bufs=8))
+        gpool = ctx.enter_context(tc.tile_pool(name="gpool", bufs=4))
+        cpool = ctx.enter_context(tc.tile_pool(name="cpool", bufs=5))
         opool = ctx.enter_context(tc.tile_pool(name="opool", bufs=4))
         psc = ctx.enter_context(tc.psum_pool(name="psc", bufs=NSC))
         pso = ctx.enter_context(tc.psum_pool(name="pso", bufs=1))
@@ -137,15 +142,17 @@ def tile_model_kernel(tc, qk, qk_scaling_factor, query, key, value, out):
         def value_regroup(b):
             vgrp = vpool.tile([P, PASSES, DV, PACK], BF16, name="vgrp", tag="vgrp", align_bytes=64)
             if REGROUP == "G":
+                step_w = DV // GP_PIECES
                 for c in range(PASSES):
-                    nc.gpsimd.tensor_scalar(
-                        out=vgrp[:, c, :, :],
-                        in0=value_sb[b][:, c, :, :].rearrange("p t w -> p w t"),
-                        scalar1=1.0,
-                        scalar2=0.0,
-                        op0=MULT,
-                        op1=ADD,
-                    )
+                    for w0 in range(0, DV, step_w):
+                        nc.gpsimd.tensor_scalar(
+                            out=vgrp[:, c, w0 : w0 + step_w, :],
+                            in0=value_sb[b][:, c, :, w0 : w0 + step_w].rearrange("p t w -> p w t"),
+                            scalar1=1.0,
+                            scalar2=0.0,
+                            op0=MULT,
+                            op1=ADD,
+                        )
             else:
                 nc.vector.tensor_copy(
                     out=vgrp[:], in_=value_sb[b][:].rearrange("p c t w -> p c w t")
@@ -164,6 +171,10 @@ def tile_model_kernel(tc, qk, qk_scaling_factor, query, key, value, out):
         new_transposed(0)
         sf_gain = const.tile([P, 1], F32, name="sf_gain")
         inv = const.tile([P, 1], F32, name="inv")
+        if VMUL == "TT":
+            ones = const.tile([P, P, PACK], F32, name="ones")
+            inv_wide = const.tile([P, P, PACK], F32, name="inv_wide")
+            nc.vector.memset(ones[:], 1.0)
         head_jobs = (
             tr_job("k", 0, 0, 4, "V", True),
             tr_job("q", 0, 0, 4, "S", True),
@@ -178,6 +189,10 @@ def tile_model_kernel(tc, qk, qk_scaling_factor, query, key, value, out):
                     out=sf_gain[:], in0=sf_raw[:], scalar1=math.sqrt(D), scalar2=None, op0=MULT
                 )
                 nc.vector.reciprocal(out=inv[:], in_=sf_gain[:])
+                if VMUL == "TT":
+                    nc.vector.tensor_scalar(
+                        out=inv_wide[:], in0=ones[:], scalar1=inv[:, 0:1], scalar2=None, op0=MULT
+                    )
 
         grp, codes, scl = {}, {}, {}
         pending_out = []
@@ -194,8 +209,8 @@ def tile_model_kernel(tc, qk, qk_scaling_factor, query, key, value, out):
                     job = tr_job("q", 0, 4, 8, "S", False)
                 elif u == 1:
                     job = tr_job("q", 0, 8, 16, "S", False)
-                elif b + 1 < B and r in JOB_AT:
-                    part = JOB_AT.index(r)
+                elif b + 1 < B and r in (JOB_AT_FIRST if b == 0 else JOB_AT):
+                    part = (JOB_AT_FIRST if b == 0 else JOB_AT).index(r)
                     eng = "S" if (part == 1 and b % 2 == 1) else "V"
                     if part == 0:
                         new_transposed(b + 1)
@@ -224,16 +239,20 @@ def tile_model_kernel(tc, qk, qk_scaling_factor, query, key, value, out):
                     if not WEAVE and jj == 1:
                         for step in todo:
                             one_transpose(step)
-                grp[u] = gpool.tile([P, QGROUP, P, PACK], BF16, name="grp", tag="grp", align_bytes=64)
-                on_vector = (0, 2) if u < K1 else (0,)
+                if c == 0:
+                    grp[u // PASSES] = gpool.tile(
+                        [P, PASSES, QGROUP, P, PACK], BF16, name="grp", tag="grp", align_bytes=64
+                    )
+                on_vector = (0, 2) if (u < K1 or u % V2_EVERY == V2_EVERY - 1) else (0,)
                 for jj in range(QGROUP):
                     src = banks[jj][:].rearrange("p t q -> p q t")
-                    if jj in on_vector:
-                        nc.vector.tensor_scalar(
-                            out=grp[u][:, jj, :, :], in0=src, scalar1=inv[:, 0:1], scalar2=None, op0=MULT
-                        )
+                    dst = grp[u // PASSES][:, c, jj, :, :]
+                    if jj in on_vector and VMUL == "TT":
+                        nc.vector.tensor_tensor(out=dst, in0=src, in1=inv_wide[:], op=MULT)
+                    elif jj in on_vector:
+                        nc.vector.tensor_scalar(out=dst, in0=src, scalar1=inv[:, 0:1], scalar2=None, op0=MULT)
                     else:
-                        nc.scalar.activation(out=grp[u][:, jj, :, :], in_=src, func=COPY, scale=inv[:, 0:1])
+                        nc.scalar.activation(out=dst, in_=src, func=COPY, scale=inv[:, 0:1])
                     if job is not None and jj == TRX_POS:
                         copy_on(*job[1])
                 if r == 3 and b + 1 < B:
@@ -251,16 +270,23 @@ def tile_model_kernel(tc, qk, qk_scaling_factor, query, key, value, out):
 
             if 1 <= u <= UNITS:
                 q = u - 1
-                codes[q] = cpool.tile([P, QGROUP * P], U32, name="codes", tag="codes", align_bytes=64)
-                scl[q] = cpool.tile([P, QGROUP * P], U8, name="scl", tag="scl", align_bytes=64)
-                pieces = QGROUP if q >= UNITS - TAIL_FINE else 1
-                width = QGROUP * P // pieces
-                for i in range(pieces):
-                    cols = slice(i * width, (i + 1) * width)
+                G = q // PASSES
+                last_group = G == B * GROUPS - 1
+                UW = QGROUP * P
+                if q % PASSES == 0:
+                    codes[G] = cpool.tile([P, PASSES * UW], U32, name="codes", tag="codes", align_bytes=64)
+                    scl[G] = cpool.tile([P, PASSES * UW], U8, name="scl", tag="scl", align_bytes=64)
+                if QWIDE and not last_group:
+                    spans = [(0, PASSES * UW)] if q % PASSES == PASSES - 1 else []
+                elif q >= UNITS - TAIL_FINE:
+                    spans = [((q % PASSES) * UW + i * P, (q % PASSES) * UW + (i + 1) * P) for i in range(QGROUP)]
+                else:
+                    spans = [((q % PASSES) * UW, (q % PASSES + 1) * UW)]
+                for lo_w, hi_w in spans:
                     nc.vector.quantize_mx(
-                        out=codes[q][:, cols].bitcast(FP8X4),
-                        scales=scl[q][:, cols],
-                        in_=grp[q][:].rearrange("p j q t -> p (j q t)")[:, i * width * PACK : (i + 1) * width * PACK],
+                        out=codes[G][:, lo_w:hi_w].bitcast(FP8X4),
+                        scales=scl[G][:, lo_w:hi_w],
+                        in_=grp[G][:].rearrange("p c j q t -> p (c j q t)")[:, lo_w * PACK : hi_w * PACK],
                     )
             for vb, vgrp in pending_vq:
                 value_quant(vb, vgrp)
@@ -280,12 +306,12 @@ def tile_model_kernel(tc, qk, qk_scaling_factor, query, key, value, out):
                     else:
                         bank = pso.tile([P, QGROUP, DV], F32, name="ob", tag="ob")
                     for jj in range(lo, hi):
-                        cols = slice(jj * P, (jj + 1) * P)
                         for c in range(PASSES):
+                            cols = slice((c * QGROUP + jj) * P, (c * QGROUP + jj + 1) * P)
                             nc.tensor.matmul_mx(
                                 out=bank[:, jj, :],
-                                lhsT=codes[uu + c][:, cols].bitcast(FP8X4),
-                                lhsT_scale=scl[uu + c][:, cols],
+                                lhsT=codes[G][:, cols].bitcast(FP8X4),
+                                lhsT_scale=scl[G][:, cols],
                                 rhs=vcodes[gb][:, c, :].bitcast(FP8X4),
                                 rhs_scale=vscales[gb][:, c, :],
                                 start=(c == 0),

@@ -45,7 +45,7 @@ REGROUP = "G"
 GP_PIECES = 4
 QWIDE = False
 VMUL = "TT"
-V2_EVERY = 10
+V2_EVERY = 20
 
 
 def tile_model_kernel(tc, qk, qk_scaling_factor, query, key, value, out):

@@ -30,7 +30,7 @@ MULT = mybir.AluOpType.mult
 ADD = mybir.AluOpType.add
 
 PIN = True
-NSC = 6
+NSC = 8
 MXLAG = 4
 K1 = 2
 OUT_S_FROM = 30
@@ -61,8 +61,6 @@ def tile_model_kernel(tc, qk, qk_scaling_factor, query, key, value, out):
         cpool = ctx.enter_context(tc.tile_pool(name="cpool", bufs=5))
         opool = ctx.enter_context(tc.tile_pool(name="opool", bufs=4))
         psc = ctx.enter_context(tc.psum_pool(name="psc", bufs=NSC))
-        pso = ctx.enter_context(tc.psum_pool(name="pso", bufs=1))
-        ptr = ctx.enter_context(tc.psum_pool(name="ptr", bufs=1))
 
         key_sb, query_sb, value_sb = [], [], []
         for b in range(B):
@@ -119,7 +117,7 @@ def tile_model_kernel(tc, qk, qk_scaling_factor, query, key, value, out):
             if head:
                 bank = psc.tile([P, 8, P], BF16, name="trh", tag="sc")
             else:
-                bank = ptr.tile([P, 8, P], BF16, name="tr", tag="tr")
+                bank = psc.tile([P, 8, P], BF16, name="tr", tag="sc")
             steps = []
             for i in range(lo, hi):
                 if kind == "k":
@@ -304,7 +302,7 @@ def tile_model_kernel(tc, qk, qk_scaling_factor, query, key, value, out):
                     if len(parts) > 1:
                         bank = psc.tile([P, QGROUP, DV], F32, name="obl", tag="sc")
                     else:
-                        bank = pso.tile([P, QGROUP, DV], F32, name="ob", tag="ob")
+                        bank = psc.tile([P, QGROUP, DV], F32, name="ob", tag="sc")
                     for jj in range(lo, hi):
                         for c in range(PASSES):
                             cols = slice((c * QGROUP + jj) * P, (c * QGROUP + jj + 1) * P)

@@ -167,16 +167,25 @@ def tile_model_kernel(tc, qk, qk_scaling_factor, query, key, value, out):
             )
 
         new_transposed(0)
+        warm_in = const.tile([P, P], BF16, name="warm_in")
+        nc.vector.memset(warm_in[:], 0.0)
         sf_gain = const.tile([P, 1], F32, name="sf_gain")
         inv = const.tile([P, 1], F32, name="inv")
         if VMUL == "TT":
             ones = const.tile([P, P, PACK], F32, name="ones")
             inv_wide = const.tile([P, P, PACK], F32, name="inv_wide")
             nc.vector.memset(ones[:], 1.0)
+        warm_out = psc.tile([P, P], F32, name="warm_out", tag="sc")
+
+        def warm_up(n):
+            for i in range(n):
+                nc.tensor.matmul(out=warm_out[:], lhsT=warm_in[:], rhs=warm_in[:], start=True, stop=True)
+
+        warm_up(14)
         head_jobs = (
             tr_job("k", 0, 0, 4, "V", True),
-            tr_job("q", 0, 0, 4, "S", True),
-            tr_job("k", 0, 4, 8, "V", True),
+            tr_job("q", 0, 0, 1, "S", True),
+            tr_job("q", 0, 1, 4, "S", True),
         )
         for n, job in enumerate(head_jobs):
             for step in job[0]:
@@ -191,6 +200,8 @@ def tile_model_kernel(tc, qk, qk_scaling_factor, query, key, value, out):
                     nc.vector.tensor_scalar(
                         out=inv_wide[:], in0=ones[:], scalar1=inv[:, 0:1], scalar2=None, op0=MULT
                     )
+
+        warm_up(2)
 
         grp, codes, scl = {}, {}, {}
         pending_out = []
@@ -234,6 +245,10 @@ def tile_model_kernel(tc, qk, qk_scaling_factor, query, key, value, out):
                         if WEAVE and jj in (1, 2) and done < len(todo):
                             one_transpose(todo[done])
                             done += 1
+                    if u == 0 and jj == 0:
+                        late_job = tr_job("k", 0, 4, 8, "V", True)
+                        for step in late_job[0]:
+                            one_transpose(step)
                     if not WEAVE and jj == 1:
                         for step in todo:
                             one_transpose(step)
@@ -251,6 +266,8 @@ def tile_model_kernel(tc, qk, qk_scaling_factor, query, key, value, out):
                         nc.vector.tensor_scalar(out=dst, in0=src, scalar1=inv[:, 0:1], scalar2=None, op0=MULT)
                     else:
                         nc.scalar.activation(out=dst, in_=src, func=COPY, scale=inv[:, 0:1])
+                    if u == 0 and jj == 0:
+                        copy_on(*late_job[1])
                     if job is not None and jj == TRX_POS:
                         copy_on(*job[1])
                 if r == 3 and b + 1 < B:

@@ -57,9 +57,9 @@ def tile_model_kernel(tc, qk, qk_scaling_factor, query, key, value, out):
         inp = ctx.enter_context(tc.tile_pool(name="inp", bufs=1))
         tpool = ctx.enter_context(tc.tile_pool(name="tpool", bufs=2))
         vpool = ctx.enter_context(tc.tile_pool(name="vpool", bufs=3))
-        gpool = ctx.enter_context(tc.tile_pool(name="gpool", bufs=4))
-        cpool = ctx.enter_context(tc.tile_pool(name="cpool", bufs=5))
-        opool = ctx.enter_context(tc.tile_pool(name="opool", bufs=4))
+        gpool = ctx.enter_context(tc.tile_pool(name="gpool", bufs=5))
+        cpool = ctx.enter_context(tc.tile_pool(name="cpool", bufs=6))
+        opool = ctx.enter_context(tc.tile_pool(name="opool", bufs=10))
         psc = ctx.enter_context(tc.psum_pool(name="psc", bufs=NSC))
 
         key_sb, query_sb, value_sb = [], [], []

@@ -45,7 +45,6 @@ REGROUP = "G"
 GP_PIECES = 4
 QWIDE = False
 VMUL = "TT"
-V2_EVERY = 20
 
 
 def tile_model_kernel(tc, qk, qk_scaling_factor, query, key, value, out):
@@ -205,7 +204,7 @@ def tile_model_kernel(tc, qk, qk_scaling_factor, query, key, value, out):
 
         grp, codes, scl = {}, {}, {}
         pending_out = []
-        pending_vq = [(0, value_regroup(0))]
+        vgrps = {0: value_regroup(0)}
 
         for u in range(UNITS + MXLAG + 2):
             if u < UNITS:
@@ -256,7 +255,7 @@ def tile_model_kernel(tc, qk, qk_scaling_factor, query, key, value, out):
                     grp[u // PASSES] = gpool.tile(
                         [P, PASSES, QGROUP, P, PACK], BF16, name="grp", tag="grp", align_bytes=64
                     )
-                on_vector = (0, 2) if (u < K1 or u % V2_EVERY == V2_EVERY - 1) else (0,)
+                on_vector = (0, 2) if (u < K1 or (job is not None and job[1][0] == "S")) else (0,)
                 for jj in range(QGROUP):
                     src = banks[jj][:].rearrange("p t q -> p q t")
                     dst = grp[u // PASSES][:, c, jj, :, :]
@@ -271,7 +270,7 @@ def tile_model_kernel(tc, qk, qk_scaling_factor, query, key, value, out):
                     if job is not None and jj == TRX_POS:
                         copy_on(*job[1])
                 if r == 3 and b + 1 < B:
-                    pending_vq.append((b + 1, value_regroup(b + 1)))
+                    vgrps[b + 1] = value_regroup(b + 1)
 
             for G, lo, hi, bank, eng in pending_out:
                 osb = opool.tile([P, QGROUP, DV], F32, name="osb", tag="osb")
@@ -303,9 +302,8 @@ def tile_model_kernel(tc, qk, qk_scaling_factor, query, key, value, out):
                         scales=scl[G][:, lo_w:hi_w],
                         in_=grp[G][:].rearrange("p c j q t -> p (c j q t)")[:, lo_w * PACK : hi_w * PACK],
                     )
-            for vb, vgrp in pending_vq:
-                value_quant(vb, vgrp)
-            pending_vq = []
+            if u < UNITS and r == (2 if b == 0 else 0):
+                value_quant(b, vgrps[b])
 
             uu = u - MXLAG
             if uu >= 0 and uu % PASSES == 0 and uu < UNITS:

@@ -66,7 +66,8 @@ def tile_model_kernel(tc, qk, qk_scaling_factor, query, key, value, out):
             key_sb.append(inp.tile([P, PASSES, PACK, D], BF16, name="key_sb%d" % b))
             query_sb.append(inp.tile([P, QBLOCKS, D], BF16, name="query_sb%d" % b))
             value_sb.append(inp.tile([P, PASSES, PACK, DV], BF16, name="value_sb%d" % b))
-        sf_raw = const.tile([P, 1], BF16, name="sf_raw")
+        sf_row = const.tile([P, 2], BF16, name="sf_row")
+        nc.vector.memset(sf_row[:], 0.0)
 
         def load_key(b, lo, hi):
             nc.sync.dma_start(
@@ -86,10 +87,7 @@ def tile_model_kernel(tc, qk, qk_scaling_factor, query, key, value, out):
                 in_=query[b].rearrange("(p j) d -> p j d", j=QBLOCKS)[:, lo:hi, :],
             )
 
-        nc.scalar.dma_start(
-            out=sf_raw[:],
-            in_=qk_scaling_factor.rearrange("a b -> (a b)").partition_broadcast(P),
-        )
+        nc.scalar.dma_start(out=sf_row[0:1, 0:1], in_=qk_scaling_factor)
         load_key(0, 0, 1)
         load_query(0, 0, 4)
         load_key(0, 1, 2)
@@ -156,6 +154,11 @@ def tile_model_kernel(tc, qk, qk_scaling_factor, query, key, value, out):
                 )
             return vgrp
 
+        def value_regroup_on_vector(b):
+            vgrp = vpool.tile([P, PASSES, DV, PACK], BF16, name="vgrp", tag="vgrp", align_bytes=64)
+            nc.vector.tensor_copy(out=vgrp[:], in_=value_sb[b][:].rearrange("p c t w -> p c w t"))
+            return vgrp
+
         def value_quant(b, vgrp):
             vcodes[b] = vpool.tile([P, PASSES, DV], U32, name="vcodes", tag="vcodes", align_bytes=64)
             vscales[b] = vpool.tile([P, PASSES, DV], U8, name="vscales", tag="vscales", align_bytes=64)
@@ -167,7 +170,7 @@ def tile_model_kernel(tc, qk, qk_scaling_factor, query, key, value, out):
 
         new_transposed(0)
         warm_in = const.tile([P, P], BF16, name="warm_in")
-        nc.vector.memset(warm_in[:], 0.0)
+        nc.vector.memset(warm_in[:], 1.0)
         sf_gain = const.tile([P, 1], F32, name="sf_gain")
         inv = const.tile([P, 1], F32, name="inv")
         if VMUL == "TT":
@@ -190,9 +193,10 @@ def tile_model_kernel(tc, qk, qk_scaling_factor, query, key, value, out):
             for step in job[0]:
                 one_transpose(step)
             copy_on(*job[1])
-            if n == 0:
+            if n == 1:
+                nc.tensor.matmul(out=warm_out[:, 0:2], lhsT=warm_in[:], rhs=sf_row[:], start=True, stop=True)
                 nc.vector.tensor_scalar(
-                    out=sf_gain[:], in0=sf_raw[:], scalar1=math.sqrt(D), scalar2=None, op0=MULT
+                    out=sf_gain[:], in0=warm_out[:, 0:1], scalar1=math.sqrt(D), scalar2=None, op0=MULT
                 )
                 nc.vector.reciprocal(out=inv[:], in_=sf_gain[:])
                 if VMUL == "TT":
@@ -200,11 +204,9 @@ def tile_model_kernel(tc, qk, qk_scaling_factor, query, key, value, out):
                         out=inv_wide[:], in0=ones[:], scalar1=inv[:, 0:1], scalar2=None, op0=MULT
                     )
 
-        warm_up(2)
-
         grp, codes, scl = {}, {}, {}
         pending_out = []
-        vgrps = {0: value_regroup(0)}
+        vgrps = {}
 
         for u in range(UNITS + MXLAG + 2):
             if u < UNITS:
@@ -271,6 +273,8 @@ def tile_model_kernel(tc, qk, qk_scaling_factor, query, key, value, out):
                         copy_on(*job[1])
                 if r == 3 and b + 1 < B:
                     vgrps[b + 1] = value_regroup(b + 1)
+                if u == 0:
+                    vgrps[0] = value_regroup_on_vector(0)
 
             for G, lo, hi, bank, eng in pending_out:
                 osb = opool.tile([P, QGROUP, DV], F32, name="osb", tag="osb")

from contextlib import ExitStack
import math

import concourse.mybir as mybir
from concourse.masks import make_identity

B = 8
SQ = 2048
SK = 1024
D = 128
DV = 128
FLOPS = 2 * B * SQ * SK * D + 2 * B * SQ * SK * DV

P = 128
PACK = 4
PASSES = SK // (P * PACK)
QBLOCKS = SQ // P
QGROUP = 4
GROUPS = QBLOCKS // QGROUP
UNITS = B * GROUPS * PASSES
UNITS_PER_BATCH = UNITS // B

BF16 = mybir.dt.bfloat16
F32 = mybir.dt.float32
U32 = mybir.dt.uint32
U8 = mybir.dt.uint8
FP8X4 = mybir.dt.float8_e4m3fn_x4
COPY = mybir.ActivationFunctionType.Copy
MULT = mybir.AluOpType.mult
ADD = mybir.AluOpType.add

PIN = True
NSC = 8
MXLAG = 4
K1 = 2
OUT_S_FROM = 30
TAIL_FINE = 1
WEAVE = False
TRX_POS = 1
TAIL_SPLIT = True
WARM = 0
JOB_AT = (2, 4, 6)
JOB_AT_FIRST = (2, 4, 6)
REGROUP = "G"
GP_PIECES = 4
QWIDE = False
VMUL = "TT"


def tile_model_kernel(tc, qk, qk_scaling_factor, query, key, value, out):
    nc = tc.nc
    with ExitStack() as ctx:
        if PIN:
            ctx.enter_context(tc.manual_schedule())
        const = ctx.enter_context(tc.tile_pool(name="const", bufs=1))
        inp = ctx.enter_context(tc.tile_pool(name="inp", bufs=1))
        tpool = ctx.enter_context(tc.tile_pool(name="tpool", bufs=2))
        vpool = ctx.enter_context(tc.tile_pool(name="vpool", bufs=3))
        gpool = ctx.enter_context(tc.tile_pool(name="gpool", bufs=5))
        cpool = ctx.enter_context(tc.tile_pool(name="cpool", bufs=6))
        opool = ctx.enter_context(tc.tile_pool(name="opool", bufs=10))
        psc = ctx.enter_context(tc.psum_pool(name="psc", bufs=NSC))

        key_sb, query_sb, value_sb = [], [], []
        for b in range(B):
            key_sb.append(inp.tile([P, PASSES, PACK, D], BF16, name="key_sb%d" % b))
            query_sb.append(inp.tile([P, QBLOCKS, D], BF16, name="query_sb%d" % b))
            value_sb.append(inp.tile([P, PASSES, PACK, DV], BF16, name="value_sb%d" % b))
        sf_row = const.tile([P, 2], BF16, name="sf_row")
        nc.vector.memset(sf_row[:], 0.0)

        def load_key(b, lo, hi):
            nc.sync.dma_start(
                out=key_sb[b][:, lo:hi, :, :],
                in_=key[b].rearrange("(c p t) d -> p c t d", c=PASSES, p=P, t=PACK)[:, lo:hi, :, :],
            )

        def load_value(b):
            nc.sync.dma_start(
                out=value_sb[b][:],
                in_=value[b].rearrange("(c p t) d -> p c t d", c=PASSES, p=P, t=PACK),
            )

        def load_query(b, lo, hi):
            nc.sync.dma_start(
                out=query_sb[b][:, lo:hi, :],
                in_=query[b].rearrange("(p j) d -> p j d", j=QBLOCKS)[:, lo:hi, :],
            )

        nc.scalar.dma_start(out=sf_row[0:1, 0:1], in_=qk_scaling_factor)
        load_key(0, 0, 1)
        load_query(0, 0, 4)
        load_key(0, 1, 2)
        load_value(0)
        load_query(0, 4, 8)
        load_query(0, 8, 16)
        for b in range(1, B):
            load_key(b, 0, PASSES)
            load_query(b, 0, QBLOCKS)
            load_value(b)

        ident = const.tile([P, P], BF16, name="ident")
        make_identity(nc, ident[:])

        keyT, queryT, vcodes, vscales = {}, {}, {}, {}

        def copy_on(eng, dst, src):
            if eng == "V":
                nc.vector.tensor_copy(out=dst, in_=src)
            else:
                nc.scalar.copy(out=dst, in_=src)

        def tr_job(kind, b, lo, hi, eng, head):
            if head:
                bank = psc.tile([P, 8, P], BF16, name="trh", tag="sc")
            else:
                bank = psc.tile([P, 8, P], BF16, name="tr", tag="sc")
            steps = []
            for i in range(lo, hi):
                if kind == "k":
                    steps.append((bank[:, i - lo, :], key_sb[b][:, i // PACK, i % PACK, :]))
                else:
                    steps.append((bank[:, i - lo, :], query_sb[b][:, i, :]))
            if kind == "k":
                dst = keyT[b][:, lo:hi, :]
            else:
                dst = queryT[b][:, lo:hi, :]
            return steps, (eng, dst, bank[:, 0 : hi - lo, :])

        def new_transposed(b):
            keyT[b] = tpool.tile([P, PASSES * PACK, P], BF16, name="keyT", tag="keyT")
            queryT[b] = tpool.tile([P, QBLOCKS, P], BF16, name="queryT", tag="queryT")

        def one_transpose(step):
            nc.tensor.transpose(out=step[0], in_=step[1], identity=ident[:])

        def value_regroup(b):
            vgrp = vpool.tile([P, PASSES, DV, PACK], BF16, name="vgrp", tag="vgrp", align_bytes=64)
            if REGROUP == "G":
                step_w = DV // GP_PIECES
                for c in range(PASSES):
                    for w0 in range(0, DV, step_w):
                        nc.gpsimd.tensor_scalar(
                            out=vgrp[:, c, w0 : w0 + step_w, :],
                            in0=value_sb[b][:, c, :, w0 : w0 + step_w].rearrange("p t w -> p w t"),
                            scalar1=1.0,
                            scalar2=0.0,
                            op0=MULT,
                            op1=ADD,
                        )
            else:
                nc.vector.tensor_copy(
                    out=vgrp[:], in_=value_sb[b][:].rearrange("p c t w -> p c w t")
                )
            return vgrp

        def value_regroup_on_vector(b):
            vgrp = vpool.tile([P, PASSES, DV, PACK], BF16, name="vgrp", tag="vgrp", align_bytes=64)
            nc.vector.tensor_copy(out=vgrp[:], in_=value_sb[b][:].rearrange("p c t w -> p c w t"))
            return vgrp

        def value_quant(b, vgrp):
            vcodes[b] = vpool.tile([P, PASSES, DV], U32, name="vcodes", tag="vcodes", align_bytes=64)
            vscales[b] = vpool.tile([P, PASSES, DV], U8, name="vscales", tag="vscales", align_bytes=64)
            nc.vector.quantize_mx(
                out=vcodes[b][:].rearrange("p c w -> p (c w)").bitcast(FP8X4),
                scales=vscales[b][:].rearrange("p c w -> p (c w)"),
                in_=vgrp[:].rearrange("p c w t -> p (c w t)"),
            )

        new_transposed(0)
        warm_in = const.tile([P, P], BF16, name="warm_in")
        nc.vector.memset(warm_in[:], 1.0)
        sf_gain = const.tile([P, 1], F32, name="sf_gain")
        inv = const.tile([P, 1], F32, name="inv")
        if VMUL == "TT":
            ones = const.tile([P, P, PACK], F32, name="ones")
            inv_wide = const.tile([P, P, PACK], F32, name="inv_wide")
            nc.vector.memset(ones[:], 1.0)
        warm_out = psc.tile([P, P], F32, name="warm_out", tag="sc")

        def warm_up(n):
            for i in range(n):
                nc.tensor.matmul(out=warm_out[:], lhsT=warm_in[:], rhs=warm_in[:], start=True, stop=True)

        warm_up(14)
        head_jobs = (
            tr_job("k", 0, 0, 4, "V", True),
            tr_job("q", 0, 0, 1, "S", True),
            tr_job("q", 0, 1, 4, "S", True),
        )
        for n, job in enumerate(head_jobs):
            for step in job[0]:
                one_transpose(step)
            copy_on(*job[1])
            if n == 1:
                nc.tensor.matmul(out=warm_out[:, 0:2], lhsT=warm_in[:], rhs=sf_row[:], start=True, stop=True)
                nc.vector.tensor_scalar(
                    out=sf_gain[:], in0=warm_out[:, 0:1], scalar1=math.sqrt(D), scalar2=None, op0=MULT
                )
                nc.vector.reciprocal(out=inv[:], in_=sf_gain[:])
                if VMUL == "TT":
                    nc.vector.tensor_scalar(
                        out=inv_wide[:], in0=ones[:], scalar1=inv[:, 0:1], scalar2=None, op0=MULT
                    )

        grp, codes, scl = {}, {}, {}
        pending_out = []
        vgrps = {}

        for u in range(UNITS + MXLAG + 2):
            if u < UNITS:
                b = u // UNITS_PER_BATCH
                r = u % UNITS_PER_BATCH
                g = r // PASSES
                c = r % PASSES
                job = None
                if u == 0:
                    job = tr_job("q", 0, 4, 8, "S", False)
                elif u == 1:
                    job = tr_job("q", 0, 8, 16, "S", False)
                elif b + 1 < B and r in (JOB_AT_FIRST if b == 0 else JOB_AT):
                    part = (JOB_AT_FIRST if b == 0 else JOB_AT).index(r)
                    eng = "S" if (part == 1 and b % 2 == 1) else "V"
                    if part == 0:
                        new_transposed(b + 1)
                        job = tr_job("k", b + 1, 0, 8, eng, False)
                    else:
                        job = tr_job("q", b + 1, 8 * (part - 1), 8 * part, eng, False)
                todo = []
                if job is not None:
                    todo = job[0]
                done = 0
                banks = []
                for jj in range(QGROUP):
                    sc = psc.tile([P, PACK, P], F32, name="sc", tag="sc")
                    banks.append(sc)
                    for t in range(PACK):
                        nc.tensor.matmul(
                            out=sc[:, t, :],
                            lhsT=keyT[b][:, PACK * c + t, :],
                            rhs=queryT[b][:, QGROUP * g + jj, :],
                            start=True,
                            stop=True,
                        )
                        if WEAVE and jj in (1, 2) and done < len(todo):
                            one_transpose(todo[done])
                            done += 1
                    if u == 0 and jj == 0:
                        late_job = tr_job("k", 0, 4, 8, "V", True)
                        for step in late_job[0]:
                            one_transpose(step)
                    if not WEAVE and jj == 1:
                        for step in todo:
                            one_transpose(step)
                if c == 0:
                    grp[u // PASSES] = gpool.tile(
                        [P, PASSES, QGROUP, P, PACK], BF16, name="grp", tag="grp", align_bytes=64
                    )
                on_vector = (0, 2) if (u < K1 or (job is not None and job[1][0] == "S")) else (0,)
                for jj in range(QGROUP):
                    src = banks[jj][:].rearrange("p t q -> p q t")
                    dst = grp[u // PASSES][:, c, jj, :, :]
                    if jj in on_vector and VMUL == "TT":
                        nc.vector.tensor_tensor(out=dst, in0=src, in1=inv_wide[:], op=MULT)
                    elif jj in on_vector:
                        nc.vector.tensor_scalar(out=dst, in0=src, scalar1=inv[:, 0:1], scalar2=None, op0=MULT)
                    else:
                        nc.scalar.activation(out=dst, in_=src, func=COPY, scale=inv[:, 0:1])
                    if u == 0 and jj == 0:
                        copy_on(*late_job[1])
                    if job is not None and jj == TRX_POS:
                        copy_on(*job[1])
                if r == 3 and b + 1 < B:
                    vgrps[b + 1] = value_regroup(b + 1)
                if u == 0:
                    vgrps[0] = value_regroup_on_vector(0)

            for G, lo, hi, bank, eng in pending_out:
                osb = opool.tile([P, QGROUP, DV], F32, name="osb", tag="osb")
                copy_on(eng, osb[:, lo:hi, :], bank[:, lo:hi, :])
                gb, gg = G // GROUPS, G % GROUPS
                nc.sync.dma_start(
                    out=out[gb].rearrange("(p j) d -> p j d", j=QBLOCKS)[:, QGROUP * gg + lo : QGROUP * gg + hi, :],
                    in_=osb[:, lo:hi, :],
                )
            pending_out = []

            if 1 <= u <= UNITS:
                q = u - 1
                G = q // PASSES
                last_group = G == B * GROUPS - 1
                UW = QGROUP * P
                if q % PASSES == 0:
                    codes[G] = cpool.tile([P, PASSES * UW], U32, name="codes", tag="codes", align_bytes=64)
                    scl[G] = cpool.tile([P, PASSES * UW], U8, name="scl", tag="scl", align_bytes=64)
                if QWIDE and not last_group:
                    spans = [(0, PASSES * UW)] if q % PASSES == PASSES - 1 else []
                elif q >= UNITS - TAIL_FINE:
                    spans = [((q % PASSES) * UW + i * P, (q % PASSES) * UW + (i + 1) * P) for i in range(QGROUP)]
                else:
                    spans = [((q % PASSES) * UW, (q % PASSES + 1) * UW)]
                for lo_w, hi_w in spans:
                    nc.vector.quantize_mx(
                        out=codes[G][:, lo_w:hi_w].bitcast(FP8X4),
                        scales=scl[G][:, lo_w:hi_w],
                        in_=grp[G][:].rearrange("p c j q t -> p (c j q t)")[:, lo_w * PACK : hi_w * PACK],
                    )
            if u < UNITS and r == (2 if b == 0 else 0):
                value_quant(b, vgrps[b])

            uu = u - MXLAG
            if uu >= 0 and uu % PASSES == 0 and uu < UNITS:
                G = uu // PASSES
                gb = G // GROUPS
                if TAIL_SPLIT and G == B * GROUPS - 1:
                    parts = ((0, QGROUP - 1, "V"), (QGROUP - 1, QGROUP, "S"))
                else:
                    parts = ((0, QGROUP, "S" if G >= OUT_S_FROM else "V"),)
                for lo, hi, eng in parts:
                    if len(parts) > 1:
                        bank = psc.tile([P, QGROUP, DV], F32, name="obl", tag="sc")
                    else:
                        bank = psc.tile([P, QGROUP, DV], F32, name="ob", tag="sc")
                    for jj in range(lo, hi):
                        for c in range(PASSES):
                            cols = slice((c * QGROUP + jj) * P, (c * QGROUP + jj + 1) * P)
                            nc.tensor.matmul_mx(
                                out=bank[:, jj, :],
                                lhsT=codes[G][:, cols].bitcast(FP8X4),
                                lhsT_scale=scl[G][:, cols],
                                rhs=vcodes[gb][:, c, :].bitcast(FP8X4),
                                rhs_scale=vscales[gb][:, c, :],
                                start=(c == 0),
                                stop=(c == PASSES - 1),
                            )
                    pending_out.append((G, lo, hi, bank, eng))
